import numpy as np
import ml_dtypes


def mxq(x, axis, fmt="e4m3"):
    dtype, down = {"e4m3": (ml_dtypes.float8_e4m3fn, 7), "e5m2": (ml_dtypes.float8_e5m2, 14)}[fmt]
    v = np.moveaxis(np.asarray(x, np.float32).astype(ml_dtypes.bfloat16).astype(np.float64), axis, -1)
    blocks = v.reshape(v.shape[:-1] + (-1, 32))
    amax = np.abs(blocks).max(-1, keepdims=True)
    byte = np.maximum(np.where(amax > 0, np.frexp(amax)[1] - 1 + 127, 0) - down, 1)
    scale = np.exp2(byte - 127.0)
    codes = (blocks / scale).astype(np.float32).astype(dtype).astype(np.float64)
    return np.moveaxis((codes * scale).reshape(v.shape), -1, axis)


WIDE = False


def mx_kscale(k):
    if not WIDE:
        return np.ones(k)
    levels = np.array([10, -10, 5, -5, 0])
    a = np.random.permutation(np.resize(levels, k // 512 * 4)).reshape(k // 512, 4)
    idx = np.arange(k)
    return np.exp2(a[idx // 512, idx % 128 // 32])


BF16 = ml_dtypes.bfloat16


def bf(x):
    return np.asarray(x, np.float32).astype(BF16)


def f64(x):
    return np.asarray(x).astype(np.float64)


B, S, NH, HD = 1, 512, 4, 128
H = NH * HD


def split_heads(x):
    return x.reshape(B, S, NH, HD).transpose(0, 2, 1, 3)


def setup_inputs():
    t = mx_kscale(S)
    t = t / t.max()
    kind = np.random.randint(0, 4, (B, S))
    base = np.where(kind < 2, 0.0, np.where(kind == 2, -10000.0, np.random.standard_normal((B, S))))
    return {"model_hidden_states": bf(np.random.standard_normal((B, S, H))),
            "k_hidden_states": bf(np.random.standard_normal((B, S, H))),
            "k_embeddings": bf(np.random.standard_normal((B, S, H)) * 0.15 * np.sqrt(S) / t[None, :, None]),
            "attention_mask": bf(base + np.log(t)[None, :])}


def reference(model_hidden_states, k_hidden_states, k_embeddings, attention_mask):
    q = split_heads(f64(model_hidden_states))
    k = split_heads(f64(k_hidden_states))
    v = split_heads(f64(k_embeddings))
    energy = q @ k.transpose(0, 1, 3, 2) / np.sqrt(HD)
    m = f64(attention_mask)[:, None, None, :]
    energy = np.where(m == 0, energy, m)
    e = np.exp(energy - energy.max(-1, keepdims=True))
    attn = (mxq(e, 3, "e4m3") @ mxq(v, 2, "e4m3")) / e.sum(-1, keepdims=True)
    return attn.transpose(0, 2, 1, 3).reshape(B, S, H)

@@ -1,0 +1,235 @@
+import math
+
+import concourse.mybir as mybir
+from concourse.masks import make_identity
+
+BF16 = mybir.dt.bfloat16
+F32 = mybir.dt.float32
+U32 = mybir.dt.uint32
+U8 = mybir.dt.uint8
+FP8X4 = mybir.dt.float8_e4m3fn_x4
+ALU = mybir.AluOpType
+ACT = mybir.ActivationFunctionType
+
+P = 128
+S = 512
+HEADS = 4
+HD = 128
+TOKEN_TILES = S // P
+TILES = HEADS * TOKEN_TILES
+PACK = 4
+SCALE = 1.0 / math.sqrt(HD)
+
+FLOPS = 2 * (2 * HEADS * S * S * HD)
+
+
+def tile_knnattention_s_kernel(
+    tc, model_hidden_states, k_hidden_states, k_embeddings, attention_mask, out
+):
+    nc = tc.nc
+    q_dram = model_hidden_states.flatten_outer_dims().rearrange("(t p) c -> p t c", p=P)
+    k_dram = k_hidden_states.flatten_outer_dims().rearrange("(t p) c -> p t c", p=P)
+    out_dram = out.flatten_outer_dims().rearrange("(t p) c -> p t c", p=P)
+    v_dram = k_embeddings.flatten_outer_dims().rearrange(
+        "(u p e) c -> p u (e c)", u=2, p=P, e=2
+    )
+
+    with (
+        tc.tile_pool(name="const", bufs=1) as const,
+        tc.tile_pool(name="work", bufs=4) as work,
+        tc.tile_pool(name="small", bufs=6) as small,
+        tc.psum_pool(name="psum_prep", bufs=1) as psum_prep,
+        tc.psum_pool(name="psum_s", bufs=3) as psum_s,
+        tc.psum_pool(name="psum_eT", bufs=2) as psum_eT,
+        tc.psum_pool(name="psum_acc", bufs=2) as psum_acc,
+        tc.manual_schedule(),
+    ):
+        mask_row = const.tile([P, S], BF16)
+        nc.vector.memset(mask_row[:], 0.0)
+        nc.sync.dma_start(out=mask_row[0:1, :], in_=attention_mask)
+        v_raw = const.tile([P, PACK, S], BF16)
+        nc.sync.dma_start(
+            out=v_raw[:].rearrange("p (u e) c -> p u (e c)", u=2), in_=v_dram
+        )
+        q_sb = []
+        k_sb = []
+        for h in range(HEADS):
+            head_cols = slice(h * HD, (h + 1) * HD)
+            q_h = const.tile([P, TOKEN_TILES, HD], BF16, name="q_sb%d" % h)
+            nc.sync.dma_start(out=q_h[:], in_=q_dram[:, :, head_cols])
+            q_sb.append(q_h)
+            k_h = const.tile([P, TOKEN_TILES, HD], BF16, name="k_sb%d" % h)
+            nc.sync.dma_start(out=k_h[:], in_=k_dram[:, :, head_cols])
+            k_sb.append(k_h)
+
+        ident_bf = const.tile([P, P], BF16)
+        make_identity(nc, ident_bf[:])
+        ident_f32 = const.tile([P, P], F32)
+        make_identity(nc, ident_f32[:])
+        ones = const.tile([P, P], BF16)
+        nc.vector.memset(ones[:], 1.0)
+        warm = const.tile([P, 1], F32)
+        nc.vector.memset(warm[:], 0.0)
+        nc.scalar.activation(out=warm[:], in_=warm[:], func=ACT.Exp)
+
+        mask_ps = psum_prep.tile([P, S], F32, tag="prep")
+        nc.tensor.matmul(mask_ps[:], lhsT=ones[:], rhs=mask_row[:], start=True, stop=True)
+        ident_kept = const.tile([P, TOKEN_TILES, P], BF16)
+        nc.vector.scalar_tensor_tensor(
+            out=ident_kept[:],
+            in0=mask_ps[:].rearrange("p (t j) -> p t j", t=TOKEN_TILES),
+            scalar=0.0,
+            in1=ident_bf[:].unsqueeze(1).to_broadcast([P, TOKEN_TILES, P]),
+            op0=ALU.is_equal,
+            op1=ALU.mult,
+        )
+        mask_all = const.tile([P, S], F32)
+        nc.vector.tensor_copy(out=mask_all[:], in_=mask_ps[:])
+
+        v_grouped = const.tile([P, S, PACK], BF16, align_bytes=64)
+        nc.vector.tensor_copy(out=v_grouped[:], in_=v_raw[:].rearrange("p t c -> p c t"))
+        v_codes = const.tile([P, S], U32, align_bytes=64)
+        v_scales = const.tile([P, S], U8, align_bytes=64)
+        nc.vector.quantize_mx(
+            out=v_codes[:].bitcast(FP8X4),
+            scales=v_scales[:],
+            in_=v_grouped[:].rearrange("p c t -> p (c t)"),
+        )
+
+        qT = []
+        kT = []
+
+        def turn_q(h):
+            qT_ps = psum_prep.tile([P, S], BF16, tag="prep")
+            for t in range(TOKEN_TILES):
+                nc.tensor.transpose(
+                    qT_ps[:, t * P : (t + 1) * P], q_sb[h][:, t, :], ident_bf[:]
+                )
+            qT_h = const.tile([P, S], BF16, name="qT%d" % h)
+            nc.scalar.copy(out=qT_h[:], in_=qT_ps[:])
+            qT.append(qT_h)
+
+        def turn_k(h):
+            kT_ps = psum_prep.tile([P, S], BF16, tag="prep")
+            for t in range(TOKEN_TILES):
+                nc.tensor.transpose(
+                    kT_ps[:, t * P : (t + 1) * P], k_sb[h][:, t, :], ident_kept[:, t, :]
+                )
+            kT_h = const.tile([P, S], BF16, name="kT%d" % h)
+            nc.scalar.copy(out=kT_h[:], in_=kT_ps[:])
+            kT.append(kT_h)
+
+        s_ps = {}
+        energy = {}
+        neg_max = {}
+        e_bf = {}
+        row_sum = {}
+        eT_ps = {}
+        e_grouped = {}
+        e_codes = {}
+        e_scales = {}
+        inv_sum = {}
+        acc = {}
+
+        def scores(n):
+            h, t = divmod(n, TOKEN_TILES)
+            s_ps[n] = psum_s.tile([P, S], F32, name="s_ps")
+            nc.tensor.matmul(
+                s_ps[n][:], lhsT=qT[h][:, t * P : (t + 1) * P], rhs=kT[h][:],
+                start=True, stop=True,
+            )
+
+        def replace(n):
+            energy[n] = work.tile([P, S], F32, name="energy")
+            nc.vector.scalar_tensor_tensor(
+                out=energy[n][:], in0=s_ps[n][:], scalar=SCALE, in1=mask_all[:],
+                op0=ALU.mult, op1=ALU.add,
+            )
+
+        def row_maximum(n):
+            neg_max[n] = small.tile([P, 1], F32, name="neg_max")
+            nc.vector.tensor_reduce(
+                out=neg_max[n][:], in_=energy[n][:], axis=mybir.AxisListType.X,
+                op=ALU.max, negate=True,
+            )
+
+        def exponential(n):
+            e_bf[n] = work.tile([P, S], BF16, name="e_bf")
+            row_sum[n] = small.tile([P, 1], F32, name="row_sum")
+            nc.scalar.activation(
+                out=e_bf[n][:], in_=energy[n][:], func=ACT.Exp,
+                bias=neg_max[n][:], scale=1.0, accum_out=row_sum[n][:],
+            )
+
+        def turn_e(n):
+            eT_ps[n] = psum_eT.tile([P, 2, P], F32, name="eT_ps")
+            e_words = e_bf[n][:].bitcast(F32)
+            for u in range(2):
+                nc.tensor.transpose(
+                    eT_ps[n][:, u, :], e_words[:, u * P : (u + 1) * P], ident_f32[:]
+                )
+
+        def group_e(n):
+            e_grouped[n] = work.tile([P, P * PACK], BF16, name="e_grouped", align_bytes=64)
+            nc.scalar.copy(
+                out=e_grouped[n][:].bitcast(F32).rearrange("p (q u) -> p q u", u=2),
+                in_=eT_ps[n][:].rearrange("p u q -> p q u"),
+            )
+
+        def quantise_e(n):
+            e_codes[n] = work.tile([P, P], U32, name="e_codes", align_bytes=64)
+            e_scales[n] = work.tile([P, P], U8, name="e_scales", align_bytes=64)
+            nc.vector.quantize_mx(
+                out=e_codes[n][:].bitcast(FP8X4), scales=e_scales[n][:],
+                in_=e_grouped[n][:],
+            )
+            inv_sum[n] = small.tile([P, 1], F32, name="inv_sum")
+            nc.vector.reciprocal(out=inv_sum[n][:], in_=row_sum[n][:])
+
+        def attend(n):
+            h = n // TOKEN_TILES
+            head_cols = slice(h * HD, (h + 1) * HD)
+            acc[n] = psum_acc.tile([P, HD], F32, name="acc")
+            nc.tensor.matmul_mx(
+                out=acc[n][:],
+                lhsT=e_codes[n][:].bitcast(FP8X4), lhsT_scale=e_scales[n][:],
+                rhs=v_codes[:, head_cols].bitcast(FP8X4), rhs_scale=v_scales[:, head_cols],
+                start=True, stop=True,
+            )
+
+        def divide_and_store(n):
+            h, t = divmod(n, TOKEN_TILES)
+            o_sb = work.tile([P, HD], F32, name="o_sb")
+            nc.scalar.activation(
+                out=o_sb[:], in_=acc[n][:], func=ACT.Copy, scale=inv_sum[n][:]
+            )
+            nc.sync.dma_start(out=out_dram[:, t, h * HD : (h + 1) * HD], in_=o_sb[:])
+
+        def in_range(n):
+            return 0 <= n < TILES
+
+        turn_q(0)
+        turn_k(0)
+        for n in range(-2, TILES + 3):
+            if in_range(n - 3):
+                attend(n - 3)
+            if in_range(n + 2):
+                scores(n + 2)
+            if in_range(n + 1):
+                replace(n + 1)
+            if in_range(n):
+                row_maximum(n)
+                exponential(n)
+            if in_range(n - 1):
+                turn_e(n - 1)
+                group_e(n - 1)
+            if in_range(n - 2):
+                quantise_e(n - 2)
+            if in_range(n - 3):
+                divide_and_store(n - 3)
+            next_head = n // TOKEN_TILES + 1
+            if n >= 0 and next_head < HEADS:
+                if n % TOKEN_TILES == 0:
+                    turn_q(next_head)
+                if n % TOKEN_TILES == 1:
+                    turn_k(next_head)

@@ -38,21 +38,18 @@ def tile_knnattention_s_kernel(
         tc.tile_pool(name="const", bufs=1) as const,
         tc.tile_pool(name="work", bufs=4) as work,
         tc.tile_pool(name="small", bufs=6) as small,
-        tc.psum_pool(name="psum_prep", bufs=1) as psum_prep,
+        tc.psum_pool(name="psum_prep", bufs=2) as psum_prep,
         tc.psum_pool(name="psum_s", bufs=3) as psum_s,
         tc.psum_pool(name="psum_eT", bufs=2) as psum_eT,
-        tc.psum_pool(name="psum_acc", bufs=2) as psum_acc,
+        tc.psum_pool(name="psum_acc", bufs=1) as psum_acc,
         tc.manual_schedule(),
     ):
         mask_row = const.tile([P, S], BF16)
-        nc.vector.memset(mask_row[:], 0.0)
+        nc.gpsimd.memset(mask_row[:].bitcast(F32), 0.0)
         nc.sync.dma_start(out=mask_row[0:1, :], in_=attention_mask)
-        v_raw = const.tile([P, PACK, S], BF16)
-        nc.sync.dma_start(
-            out=v_raw[:].rearrange("p (u e) c -> p u (e c)", u=2), in_=v_dram
-        )
         q_sb = []
         k_sb = []
+        v_raw = const.tile([P, PACK, S], BF16)
         for h in range(HEADS):
             head_cols = slice(h * HD, (h + 1) * HD)
             q_h = const.tile([P, TOKEN_TILES, HD], BF16, name="q_sb%d" % h)
@@ -61,6 +58,10 @@ def tile_knnattention_s_kernel(
             k_h = const.tile([P, TOKEN_TILES, HD], BF16, name="k_sb%d" % h)
             nc.sync.dma_start(out=k_h[:], in_=k_dram[:, :, head_cols])
             k_sb.append(k_h)
+            if h == 0:
+                nc.sync.dma_start(
+                    out=v_raw[:].rearrange("p (u e) c -> p u (e c)", u=2), in_=v_dram
+                )
 
         ident_bf = const.tile([P, P], BF16)
         make_identity(nc, ident_bf[:])
@@ -72,29 +73,37 @@ def tile_knnattention_s_kernel(
         nc.vector.memset(warm[:], 0.0)
         nc.scalar.activation(out=warm[:], in_=warm[:], func=ACT.Exp)
 
-        mask_ps = psum_prep.tile([P, S], F32, tag="prep")
-        nc.tensor.matmul(mask_ps[:], lhsT=ones[:], rhs=mask_row[:], start=True, stop=True)
+        mask_ps = psum_acc.tile([P, TOKEN_TILES, P], F32, tag="acc")
+        for t in range(TOKEN_TILES):
+            nc.tensor.matmul(
+                mask_ps[:, t, :], lhsT=mask_row[:, t * P : (t + 1) * P], rhs=ones[:],
+                start=True, stop=True,
+            )
         ident_kept = const.tile([P, TOKEN_TILES, P], BF16)
         nc.vector.scalar_tensor_tensor(
             out=ident_kept[:],
-            in0=mask_ps[:].rearrange("p (t j) -> p t j", t=TOKEN_TILES),
+            in0=mask_ps[:],
             scalar=0.0,
             in1=ident_bf[:].unsqueeze(1).to_broadcast([P, TOKEN_TILES, P]),
             op0=ALU.is_equal,
             op1=ALU.mult,
         )
-        mask_all = const.tile([P, S], F32)
-        nc.vector.tensor_copy(out=mask_all[:], in_=mask_ps[:])
+        mask_cols = const.tile([P, TOKEN_TILES, P], F32)
+        nc.vector.tensor_scalar_mul(out=mask_cols[:], in0=mask_ps[:], scalar1=math.sqrt(HD))
 
         v_grouped = const.tile([P, S, PACK], BF16, align_bytes=64)
-        nc.vector.tensor_copy(out=v_grouped[:], in_=v_raw[:].rearrange("p t c -> p c t"))
         v_codes = const.tile([P, S], U32, align_bytes=64)
         v_scales = const.tile([P, S], U8, align_bytes=64)
-        nc.vector.quantize_mx(
-            out=v_codes[:].bitcast(FP8X4),
-            scales=v_scales[:],
-            in_=v_grouped[:].rearrange("p c t -> p (c t)"),
-        )
+
+        def quantise_v():
+            nc.vector.tensor_copy(
+                out=v_grouped[:], in_=v_raw[:].rearrange("p t c -> p c t")
+            )
+            nc.vector.quantize_mx(
+                out=v_codes[:].bitcast(FP8X4),
+                scales=v_scales[:],
+                in_=v_grouped[:].rearrange("p c t -> p (c t)"),
+            )
 
         qT = []
         kT = []
@@ -120,7 +129,6 @@ def tile_knnattention_s_kernel(
             kT.append(kT_h)
 
         s_ps = {}
-        energy = {}
         neg_max = {}
         e_bf = {}
         row_sum = {}
@@ -136,29 +144,29 @@ def tile_knnattention_s_kernel(
             s_ps[n] = psum_s.tile([P, S], F32, name="s_ps")
             nc.tensor.matmul(
                 s_ps[n][:], lhsT=qT[h][:, t * P : (t + 1) * P], rhs=kT[h][:],
-                start=True, stop=True,
+                start=True, stop=False,
             )
-
-        def replace(n):
-            energy[n] = work.tile([P, S], F32, name="energy")
-            nc.vector.scalar_tensor_tensor(
-                out=energy[n][:], in0=s_ps[n][:], scalar=SCALE, in1=mask_all[:],
-                op0=ALU.mult, op1=ALU.add,
-            )
+            for kt in range(TOKEN_TILES):
+                nc.tensor.matmul(
+                    s_ps[n][:, kt * P : (kt + 1) * P],
+                    lhsT=mask_cols[:, kt, :], rhs=ident_f32[:], is_transpose=True,
+                    start=False, stop=(kt == TOKEN_TILES - 1),
+                )
 
         def row_maximum(n):
+            scaled = work.tile([P, S], BF16, name="scaled")
             neg_max[n] = small.tile([P, 1], F32, name="neg_max")
-            nc.vector.tensor_reduce(
-                out=neg_max[n][:], in_=energy[n][:], axis=mybir.AxisListType.X,
-                op=ALU.max, negate=True,
+            nc.vector.tensor_scalar(
+                out=scaled[:], in0=s_ps[n][:], scalar1=-SCALE, scalar2=None,
+                op0=ALU.mult, op1=ALU.min, accum_out=neg_max[n][:],
             )
 
         def exponential(n):
             e_bf[n] = work.tile([P, S], BF16, name="e_bf")
             row_sum[n] = small.tile([P, 1], F32, name="row_sum")
             nc.scalar.activation(
-                out=e_bf[n][:], in_=energy[n][:], func=ACT.Exp,
-                bias=neg_max[n][:], scale=1.0, accum_out=row_sum[n][:],
+                out=e_bf[n][:], in_=s_ps[n][:], func=ACT.Exp,
+                bias=neg_max[n][:], scale=SCALE, accum_out=row_sum[n][:],
             )
 
         def turn_e(n):
@@ -189,7 +197,7 @@ def tile_knnattention_s_kernel(
         def attend(n):
             h = n // TOKEN_TILES
             head_cols = slice(h * HD, (h + 1) * HD)
-            acc[n] = psum_acc.tile([P, HD], F32, name="acc")
+            acc[n] = psum_acc.tile([P, HD], F32, name="acc", tag="acc")
             nc.tensor.matmul_mx(
                 out=acc[n][:],
                 lhsT=e_codes[n][:].bitcast(FP8X4), lhsT_scale=e_scales[n][:],
@@ -200,36 +208,38 @@ def tile_knnattention_s_kernel(
         def divide_and_store(n):
             h, t = divmod(n, TOKEN_TILES)
             o_sb = work.tile([P, HD], F32, name="o_sb")
-            nc.scalar.activation(
-                out=o_sb[:], in_=acc[n][:], func=ACT.Copy, scale=inv_sum[n][:]
-            )
+            nc.vector.tensor_scalar_mul(out=o_sb[:], in0=acc[n][:], scalar1=inv_sum[n][:])
             nc.sync.dma_start(out=out_dram[:, t, h * HD : (h + 1) * HD], in_=o_sb[:])
 
         def in_range(n):
             return 0 <= n < TILES
 
+        def pipeline_round(r):
+            if in_range(r - 3):
+                attend(r - 3)
+            if in_range(r + 1):
+                scores(r + 1)
+            if in_range(r):
+                row_maximum(r)
+                exponential(r)
+            if in_range(r - 1):
+                turn_e(r - 1)
+                group_e(r - 1)
+            if in_range(r - 3):
+                divide_and_store(r - 3)
+            if in_range(r - 2):
+                quantise_e(r - 2)
+            next_head = r // TOKEN_TILES + 1
+            if r >= 0 and next_head < HEADS:
+                if r % TOKEN_TILES == 0:
+                    turn_q(next_head)
+                if r % TOKEN_TILES == 1:
+                    turn_k(next_head)
+
         turn_q(0)
         turn_k(0)
-        for n in range(-2, TILES + 3):
-            if in_range(n - 3):
-                attend(n - 3)
-            if in_range(n + 2):
-                scores(n + 2)
-            if in_range(n + 1):
-                replace(n + 1)
-            if in_range(n):
-                row_maximum(n)
-                exponential(n)
-            if in_range(n - 1):
-                turn_e(n - 1)
-                group_e(n - 1)
-            if in_range(n - 2):
-                quantise_e(n - 2)
-            if in_range(n - 3):
-                divide_and_store(n - 3)
-            next_head = n // TOKEN_TILES + 1
-            if n >= 0 and next_head < HEADS:
-                if n % TOKEN_TILES == 0:
-                    turn_q(next_head)
-                if n % TOKEN_TILES == 1:
-                    turn_k(next_head)
+        pipeline_round(-1)
+        pipeline_round(0)
+        quantise_v()
+        for r in range(1, TILES + 3):
+            pipeline_round(r)

@@ -19,6 +19,7 @@ TOKEN_TILES = S // P
 TILES = HEADS * TOKEN_TILES
 PACK = 4
 SCALE = 1.0 / math.sqrt(HD)
+V_ROUND = 2
 
 FLOPS = 2 * (2 * HEADS * S * S * HD)
 
@@ -37,11 +38,11 @@ def tile_knnattention_s_kernel(
     with (
         tc.tile_pool(name="const", bufs=1) as const,
         tc.tile_pool(name="work", bufs=4) as work,
-        tc.tile_pool(name="small", bufs=6) as small,
-        tc.psum_pool(name="psum_prep", bufs=2) as psum_prep,
+        tc.tile_pool(name="small", bufs=8) as small,
+        tc.psum_pool(name="psum_prep", bufs=1) as psum_prep,
         tc.psum_pool(name="psum_s", bufs=3) as psum_s,
         tc.psum_pool(name="psum_eT", bufs=2) as psum_eT,
-        tc.psum_pool(name="psum_acc", bufs=1) as psum_acc,
+        tc.psum_pool(name="psum_acc", bufs=2) as psum_acc,
         tc.manual_schedule(),
     ):
         mask_row = const.tile([P, S], BF16)
@@ -215,31 +216,32 @@ def tile_knnattention_s_kernel(
             return 0 <= n < TILES
 
         def pipeline_round(r):
-            if in_range(r - 3):
-                attend(r - 3)
-            if in_range(r + 1):
-                scores(r + 1)
+            if in_range(r - 6):
+                attend(r - 6)
             if in_range(r):
-                row_maximum(r)
-                exponential(r)
+                scores(r)
             if in_range(r - 1):
-                turn_e(r - 1)
-                group_e(r - 1)
-            if in_range(r - 3):
-                divide_and_store(r - 3)
+                row_maximum(r - 1)
             if in_range(r - 2):
-                quantise_e(r - 2)
+                exponential(r - 2)
+            if in_range(r - 3):
+                turn_e(r - 3)
+            if in_range(r - 4):
+                group_e(r - 4)
+            if in_range(r - 7):
+                divide_and_store(r - 7)
+            if in_range(r - 5):
+                quantise_e(r - 5)
             next_head = r // TOKEN_TILES + 1
-            if r >= 0 and next_head < HEADS:
-                if r % TOKEN_TILES == 0:
-                    turn_q(next_head)
+            if next_head < HEADS:
                 if r % TOKEN_TILES == 1:
+                    turn_q(next_head)
+                if r % TOKEN_TILES == 2:
                     turn_k(next_head)
 
         turn_q(0)
         turn_k(0)
-        pipeline_round(-1)
-        pipeline_round(0)
-        quantise_v()
-        for r in range(1, TILES + 3):
+        for r in range(TILES + 8):
             pipeline_round(r)
+            if r == V_ROUND:
+                quantise_v()

@@ -18,6 +18,7 @@ HD = 128
 TOKEN_TILES = S // P
 TILES = HEADS * TOKEN_TILES
 PACK = 4
+PAIR = 2
 SCALE = 1.0 / math.sqrt(HD)
 V_ROUND = 2
 
@@ -163,61 +164,81 @@ def tile_knnattention_s_kernel(
             )
 
         def exponential(n):
+            m, j = divmod(n, PAIR)
+            if j == 0:
+                row_sum[m] = small.tile([P, PAIR], F32, name="row_sum")
             e_bf[n] = work.tile([P, S], BF16, name="e_bf")
-            row_sum[n] = small.tile([P, 1], F32, name="row_sum")
             nc.scalar.activation(
                 out=e_bf[n][:], in_=s_ps[n][:], func=ACT.Exp,
-                bias=neg_max[n][:], scale=SCALE, accum_out=row_sum[n][:],
+                bias=neg_max[n][:], scale=SCALE, accum_out=row_sum[m][:, j : j + 1],
             )
 
         def turn_e(n):
-            eT_ps[n] = psum_eT.tile([P, 2, P], F32, name="eT_ps")
+            m, j = divmod(n, PAIR)
+            if j == 0:
+                eT_ps[m] = psum_eT.tile([P, PAIR, 2, P], F32, name="eT_ps")
             e_words = e_bf[n][:].bitcast(F32)
             for u in range(2):
                 nc.tensor.transpose(
-                    eT_ps[n][:, u, :], e_words[:, u * P : (u + 1) * P], ident_f32[:]
+                    eT_ps[m][:, j, u, :], e_words[:, u * P : (u + 1) * P], ident_f32[:]
                 )
 
-        def group_e(n):
-            e_grouped[n] = work.tile([P, P * PACK], BF16, name="e_grouped", align_bytes=64)
+        def group_e(m):
+            e_grouped[m] = work.tile(
+                [P, PAIR * P * PACK], BF16, name="e_grouped", align_bytes=64
+            )
             nc.scalar.copy(
-                out=e_grouped[n][:].bitcast(F32).rearrange("p (q u) -> p q u", u=2),
-                in_=eT_ps[n][:].rearrange("p u q -> p q u"),
+                out=e_grouped[m][:].bitcast(F32).rearrange(
+                    "p (j q u) -> p j q u", j=PAIR, u=2
+                ),
+                in_=eT_ps[m][:].rearrange("p j u q -> p j q u"),
             )
 
-        def quantise_e(n):
-            e_codes[n] = work.tile([P, P], U32, name="e_codes", align_bytes=64)
-            e_scales[n] = work.tile([P, P], U8, name="e_scales", align_bytes=64)
+        def quantise_e(m):
+            e_codes[m] = work.tile([P, PAIR * P], U32, name="e_codes", align_bytes=64)
+            e_scales[m] = work.tile([P, PAIR * P], U8, name="e_scales", align_bytes=64)
             nc.vector.quantize_mx(
-                out=e_codes[n][:].bitcast(FP8X4), scales=e_scales[n][:],
-                in_=e_grouped[n][:],
+                out=e_codes[m][:].bitcast(FP8X4), scales=e_scales[m][:],
+                in_=e_grouped[m][:],
             )
-            inv_sum[n] = small.tile([P, 1], F32, name="inv_sum")
-            nc.vector.reciprocal(out=inv_sum[n][:], in_=row_sum[n][:])
+            inv_sum[m] = small.tile([P, PAIR], F32, name="inv_sum")
+            nc.vector.reciprocal(out=inv_sum[m][:], in_=row_sum[m][:])
 
-        def attend(n):
-            h = n // TOKEN_TILES
+        def attend(m):
+            h = (m * PAIR) // TOKEN_TILES
             head_cols = slice(h * HD, (h + 1) * HD)
-            acc[n] = psum_acc.tile([P, HD], F32, name="acc", tag="acc")
-            nc.tensor.matmul_mx(
-                out=acc[n][:],
-                lhsT=e_codes[n][:].bitcast(FP8X4), lhsT_scale=e_scales[n][:],
-                rhs=v_codes[:, head_cols].bitcast(FP8X4), rhs_scale=v_scales[:, head_cols],
-                start=True, stop=True,
-            )
+            acc[m] = psum_acc.tile([P, PAIR, HD], F32, name="acc", tag="acc")
+            for j in range(PAIR):
+                queries = slice(j * P, (j + 1) * P)
+                nc.tensor.matmul_mx(
+                    out=acc[m][:, j, :],
+                    lhsT=e_codes[m][:, queries].bitcast(FP8X4),
+                    lhsT_scale=e_scales[m][:, queries],
+                    rhs=v_codes[:, head_cols].bitcast(FP8X4),
+                    rhs_scale=v_scales[:, head_cols],
+                    start=True, stop=True,
+                )
 
-        def divide_and_store(n):
-            h, t = divmod(n, TOKEN_TILES)
-            o_sb = work.tile([P, HD], F32, name="o_sb")
-            nc.vector.tensor_scalar_mul(out=o_sb[:], in0=acc[n][:], scalar1=inv_sum[n][:])
-            nc.sync.dma_start(out=out_dram[:, t, h * HD : (h + 1) * HD], in_=o_sb[:])
+        def divide_and_store(m):
+            h, t = divmod(m * PAIR, TOKEN_TILES)
+            o_sb = work.tile([P, PAIR, HD], F32, name="o_sb")
+            nc.vector.tensor_tensor(
+                out=o_sb[:], in0=acc[m][:],
+                in1=inv_sum[m][:].unsqueeze(2).to_broadcast([P, PAIR, HD]), op=ALU.mult,
+            )
+            nc.sync.dma_start(
+                out=out_dram[:, t : t + PAIR, h * HD : (h + 1) * HD], in_=o_sb[:]
+            )
 
         def in_range(n):
             return 0 <= n < TILES
 
+        def ends_pair(n):
+            return in_range(n) and n % PAIR == PAIR - 1
+
         def pipeline_round(r):
-            if in_range(r - 6):
-                attend(r - 6)
+            if ends_pair(r - 6):
+                attend((r - 6) // PAIR)
             if in_range(r):
                 scores(r)
             if in_range(r - 1):
@@ -226,12 +247,12 @@ def tile_knnattention_s_kernel(
                 exponential(r - 2)
             if in_range(r - 3):
                 turn_e(r - 3)
-            if in_range(r - 4):
-                group_e(r - 4)
-            if in_range(r - 7):
-                divide_and_store(r - 7)
-            if in_range(r - 5):
-                quantise_e(r - 5)
+            if ends_pair(r - 4):
+                group_e((r - 4) // PAIR)
+            if ends_pair(r - 8):
+                divide_and_store((r - 8) // PAIR)
+            if ends_pair(r - 5):
+                quantise_e((r - 5) // PAIR)
             next_head = r // TOKEN_TILES + 1
             if next_head < HEADS:
                 if r % TOKEN_TILES == 1:
@@ -241,7 +262,7 @@ def tile_knnattention_s_kernel(
 
         turn_q(0)
         turn_k(0)
-        for r in range(TILES + 8):
+        for r in range(TILES + 9):
             pipeline_round(r)
             if r == V_ROUND:
                 quantise_v()

import math

import concourse.mybir as mybir
from concourse.masks import make_identity

BF16 = mybir.dt.bfloat16
F32 = mybir.dt.float32
U32 = mybir.dt.uint32
U8 = mybir.dt.uint8
FP8X4 = mybir.dt.float8_e4m3fn_x4
ALU = mybir.AluOpType
ACT = mybir.ActivationFunctionType

P = 128
S = 512
HEADS = 4
HD = 128
TOKEN_TILES = S // P
TILES = HEADS * TOKEN_TILES
PACK = 4
PAIR = 2
SCALE = 1.0 / math.sqrt(HD)
V_ROUND = 2

FLOPS = 2 * (2 * HEADS * S * S * HD)


def tile_knnattention_s_kernel(
    tc, model_hidden_states, k_hidden_states, k_embeddings, attention_mask, out
):
    nc = tc.nc
    q_dram = model_hidden_states.flatten_outer_dims().rearrange("(t p) c -> p t c", p=P)
    k_dram = k_hidden_states.flatten_outer_dims().rearrange("(t p) c -> p t c", p=P)
    out_dram = out.flatten_outer_dims().rearrange("(t p) c -> p t c", p=P)
    v_dram = k_embeddings.flatten_outer_dims().rearrange(
        "(u p e) c -> p u (e c)", u=2, p=P, e=2
    )

    with (
        tc.tile_pool(name="const", bufs=1) as const,
        tc.tile_pool(name="work", bufs=4) as work,
        tc.tile_pool(name="small", bufs=8) as small,
        tc.psum_pool(name="psum_prep", bufs=1) as psum_prep,
        tc.psum_pool(name="psum_s", bufs=3) as psum_s,
        tc.psum_pool(name="psum_eT", bufs=2) as psum_eT,
        tc.psum_pool(name="psum_acc", bufs=2) as psum_acc,
        tc.manual_schedule(),
    ):
        mask_row = const.tile([P, S], BF16)
        nc.gpsimd.memset(mask_row[:].bitcast(F32), 0.0)
        nc.sync.dma_start(out=mask_row[0:1, :], in_=attention_mask)
        q_sb = []
        k_sb = []
        v_raw = const.tile([P, PACK, S], BF16)
        for h in range(HEADS):
            head_cols = slice(h * HD, (h + 1) * HD)
            q_h = const.tile([P, TOKEN_TILES, HD], BF16, name="q_sb%d" % h)
            nc.sync.dma_start(out=q_h[:], in_=q_dram[:, :, head_cols])
            q_sb.append(q_h)
            k_h = const.tile([P, TOKEN_TILES, HD], BF16, name="k_sb%d" % h)
            nc.sync.dma_start(out=k_h[:], in_=k_dram[:, :, head_cols])
            k_sb.append(k_h)
            if h == 0:
                nc.sync.dma_start(
                    out=v_raw[:].rearrange("p (u e) c -> p u (e c)", u=2), in_=v_dram
                )

        ident_bf = const.tile([P, P], BF16)
        make_identity(nc, ident_bf[:])
        ident_f32 = const.tile([P, P], F32)
        make_identity(nc, ident_f32[:])
        ones = const.tile([P, P], BF16)
        nc.vector.memset(ones[:], 1.0)
        warm = const.tile([P, 1], F32)
        nc.vector.memset(warm[:], 0.0)
        nc.scalar.activation(out=warm[:], in_=warm[:], func=ACT.Exp)

        mask_ps = psum_acc.tile([P, TOKEN_TILES, P], F32, tag="acc")
        for t in range(TOKEN_TILES):
            nc.tensor.matmul(
                mask_ps[:, t, :], lhsT=mask_row[:, t * P : (t + 1) * P], rhs=ones[:],
                start=True, stop=True,
            )
        ident_kept = const.tile([P, TOKEN_TILES, P], BF16)
        nc.vector.scalar_tensor_tensor(
            out=ident_kept[:],
            in0=mask_ps[:],
            scalar=0.0,
            in1=ident_bf[:].unsqueeze(1).to_broadcast([P, TOKEN_TILES, P]),
            op0=ALU.is_equal,
            op1=ALU.mult,
        )
        mask_cols = const.tile([P, TOKEN_TILES, P], F32)
        nc.vector.tensor_scalar_mul(out=mask_cols[:], in0=mask_ps[:], scalar1=math.sqrt(HD))

        v_grouped = const.tile([P, S, PACK], BF16, align_bytes=64)
        v_codes = const.tile([P, S], U32, align_bytes=64)
        v_scales = const.tile([P, S], U8, align_bytes=64)

        def quantise_v():
            nc.vector.tensor_copy(
                out=v_grouped[:], in_=v_raw[:].rearrange("p t c -> p c t")
            )
            nc.vector.quantize_mx(
                out=v_codes[:].bitcast(FP8X4),
                scales=v_scales[:],
                in_=v_grouped[:].rearrange("p c t -> p (c t)"),
            )

        qT = []
        kT = []

        def turn_q(h):
            qT_ps = psum_prep.tile([P, S], BF16, tag="prep")
            for t in range(TOKEN_TILES):
                nc.tensor.transpose(
                    qT_ps[:, t * P : (t + 1) * P], q_sb[h][:, t, :], ident_bf[:]
                )
            qT_h = const.tile([P, S], BF16, name="qT%d" % h)
            nc.scalar.copy(out=qT_h[:], in_=qT_ps[:])
            qT.append(qT_h)

        def turn_k(h):
            kT_ps = psum_prep.tile([P, S], BF16, tag="prep")
            for t in range(TOKEN_TILES):
                nc.tensor.transpose(
                    kT_ps[:, t * P : (t + 1) * P], k_sb[h][:, t, :], ident_kept[:, t, :]
                )
            kT_h = const.tile([P, S], BF16, name="kT%d" % h)
            nc.scalar.copy(out=kT_h[:], in_=kT_ps[:])
            kT.append(kT_h)

        s_ps = {}
        neg_max = {}
        e_bf = {}
        row_sum = {}
        eT_ps = {}
        e_grouped = {}
        e_codes = {}
        e_scales = {}
        inv_sum = {}
        acc = {}

        def scores(n):
            h, t = divmod(n, TOKEN_TILES)
            s_ps[n] = psum_s.tile([P, S], F32, name="s_ps")
            nc.tensor.matmul(
                s_ps[n][:], lhsT=qT[h][:, t * P : (t + 1) * P], rhs=kT[h][:],
                start=True, stop=False,
            )
            for kt in range(TOKEN_TILES):
                nc.tensor.matmul(
                    s_ps[n][:, kt * P : (kt + 1) * P],
                    lhsT=mask_cols[:, kt, :], rhs=ident_f32[:], is_transpose=True,
                    start=False, stop=(kt == TOKEN_TILES - 1),
                )

        def row_maximum(n):
            scaled = work.tile([P, S], BF16, name="scaled")
            neg_max[n] = small.tile([P, 1], F32, name="neg_max")
            nc.vector.tensor_scalar(
                out=scaled[:], in0=s_ps[n][:], scalar1=-SCALE, scalar2=None,
                op0=ALU.mult, op1=ALU.min, accum_out=neg_max[n][:],
            )

        def exponential(n):
            m, j = divmod(n, PAIR)
            if j == 0:
                row_sum[m] = small.tile([P, PAIR], F32, name="row_sum")
            e_bf[n] = work.tile([P, S], BF16, name="e_bf")
            nc.scalar.activation(
                out=e_bf[n][:], in_=s_ps[n][:], func=ACT.Exp,
                bias=neg_max[n][:], scale=SCALE, accum_out=row_sum[m][:, j : j + 1],
            )

        def turn_e(n):
            m, j = divmod(n, PAIR)
            if j == 0:
                eT_ps[m] = psum_eT.tile([P, PAIR, 2, P], F32, name="eT_ps")
            e_words = e_bf[n][:].bitcast(F32)
            for u in range(2):
                nc.tensor.transpose(
                    eT_ps[m][:, j, u, :], e_words[:, u * P : (u + 1) * P], ident_f32[:]
                )

        def group_e(m):
            e_grouped[m] = work.tile(
                [P, PAIR * P * PACK], BF16, name="e_grouped", align_bytes=64
            )
            nc.scalar.copy(
                out=e_grouped[m][:].bitcast(F32).rearrange(
                    "p (j q u) -> p j q u", j=PAIR, u=2
                ),
                in_=eT_ps[m][:].rearrange("p j u q -> p j q u"),
            )

        def quantise_e(m):
            e_codes[m] = work.tile([P, PAIR * P], U32, name="e_codes", align_bytes=64)
            e_scales[m] = work.tile([P, PAIR * P], U8, name="e_scales", align_bytes=64)
            nc.vector.quantize_mx(
                out=e_codes[m][:].bitcast(FP8X4), scales=e_scales[m][:],
                in_=e_grouped[m][:],
            )
            inv_sum[m] = small.tile([P, PAIR], F32, name="inv_sum")
            nc.vector.reciprocal(out=inv_sum[m][:], in_=row_sum[m][:])

        def attend(m):
            h = (m * PAIR) // TOKEN_TILES
            head_cols = slice(h * HD, (h + 1) * HD)
            acc[m] = psum_acc.tile([P, PAIR, HD], F32, name="acc", tag="acc")
            for j in range(PAIR):
                queries = slice(j * P, (j + 1) * P)
                nc.tensor.matmul_mx(
                    out=acc[m][:, j, :],
                    lhsT=e_codes[m][:, queries].bitcast(FP8X4),
                    lhsT_scale=e_scales[m][:, queries],
                    rhs=v_codes[:, head_cols].bitcast(FP8X4),
                    rhs_scale=v_scales[:, head_cols],
                    start=True, stop=True,
                )

        def divide_and_store(m):
            h, t = divmod(m * PAIR, TOKEN_TILES)
            o_sb = work.tile([P, PAIR, HD], F32, name="o_sb")
            nc.vector.tensor_tensor(
                out=o_sb[:], in0=acc[m][:],
                in1=inv_sum[m][:].unsqueeze(2).to_broadcast([P, PAIR, HD]), op=ALU.mult,
            )
            nc.sync.dma_start(
                out=out_dram[:, t : t + PAIR, h * HD : (h + 1) * HD], in_=o_sb[:]
            )

        def in_range(n):
            return 0 <= n < TILES

        def ends_pair(n):
            return in_range(n) and n % PAIR == PAIR - 1

        def pipeline_round(r):
            if ends_pair(r - 6):
                attend((r - 6) // PAIR)
            if in_range(r):
                scores(r)
            if in_range(r - 1):
                row_maximum(r - 1)
            if in_range(r - 2):
                exponential(r - 2)
            if in_range(r - 3):
                turn_e(r - 3)
            if ends_pair(r - 4):
                group_e((r - 4) // PAIR)
            if ends_pair(r - 8):
                divide_and_store((r - 8) // PAIR)
            if ends_pair(r - 5):
                quantise_e((r - 5) // PAIR)
            next_head = r // TOKEN_TILES + 1
            if next_head < HEADS:
                if r % TOKEN_TILES == 1:
                    turn_q(next_head)
                if r % TOKEN_TILES == 2:
                    turn_k(next_head)

        turn_q(0)
        turn_k(0)
        for r in range(TILES + 9):
            pipeline_round(r)
            if r == V_ROUND:
                quantise_v()
